import numpy as np
import ml_dtypes

BF16 = ml_dtypes.bfloat16


def bf(x):
    return np.asarray(x, np.float32).astype(BF16)


def f32(x):
    return np.asarray(x, np.float32)


def f64(x):
    return np.asarray(x).astype(np.float64)


def striped(idx):
    return np.tile(idx.reshape(-1, 16).T, (8, 1))


C, H, HD, S, N = 512, 4, 128, 4096, 1024
EPS = 1e-5


def setup_inputs():
    rn = np.random.standard_normal
    return {
        "wte": f32(rn((C, S))),
        "wpe": f32(rn((C, N))),
        "ln_gain": f32(1.0 + 0.1 * rn((C, 1))),
        "ln_bias": f32(0.1 * rn((C, 1))),
        "wq": bf(rn((C, C)) * np.sqrt(2.0 / C)),
        "bq": f32(0.1 * rn((C, 1))),
        "wk": bf(rn((C, C)) * np.sqrt(2.0 / C)),
        "wv": bf(rn((C, C)) / np.sqrt(C)),
        "bv": f32(0.1 * rn((C, 1))),
        "wo": bf(2.0 * rn((C, C)) / np.sqrt(C)),
        "gate": f32(np.repeat(0.5 + np.random.random_sample((H, 1)), HD, axis=0)),
        "offs": striped(np.random.permutation(np.tile(np.arange(S), 2))[:N]),
    }


def reference(wte, wpe, ln_gain, ln_bias, wq, bq, wk, wv, bv, wo, gate, offs):
    idx = offs[:16].T.reshape(-1)
    h = f64(wte)[:, idx] + f64(wpe)
    mu = h.mean(axis=0, keepdims=True)
    var = ((h - mu) ** 2).mean(axis=0, keepdims=True)
    x = (h - mu) / np.sqrt(var + EPS) * f64(ln_gain) + f64(ln_bias)
    q = (f64(wq).T @ x + f64(bq)).reshape(H, HD, N)
    k = (f64(wk).T @ x).reshape(H, HD, N)
    v = (f64(wv).T @ x + f64(bv)).reshape(H, HD, N)
    sc = np.einsum("nej,nei->nji", q, k) / np.sqrt(HD)
    keep = np.tril(np.ones((N, N)))
    e = np.exp(sc - sc.max(axis=2, keepdims=True)) * keep
    a = e / e.sum(axis=2, keepdims=True)
    o = np.einsum("nji,nei->nej", a, v).reshape(C, N)
    return h + f64(wo).T @ (f64(gate) * o)

@@ -1,0 +1,301 @@
+import math
+
+import concourse.mybir as mybir
+from concourse.masks import make_identity
+
+F32 = mybir.dt.float32
+BF16 = mybir.dt.bfloat16
+U16 = mybir.dt.uint16
+ALU = mybir.AluOpType
+ACT = mybir.ActivationFunctionType
+
+P = 128
+C = 512
+CB = C // P
+H = 4
+S = 4096
+N = 1024
+JB = N // P
+BANK = 512
+EPS = 1e-5
+SCORE_SCALE = 1.0 / math.sqrt(P)
+MASKED = -1.0e30
+
+FLOPS = 4 * 2 * C * C * N + 2 * 2 * P * H * (N * (N + 1) // 2)
+
+
+def blocks(ap, n):
+    return ap.rearrange("p (a f) -> p a f", a=n)
+
+
+def tile_adaptivetransformermodel_b_kernel(
+    tc, wte, wpe, ln_gain, ln_bias, wq, bq, wk, wv, bv, wo, gate, offs, out
+):
+    nc = tc.nc
+    with (
+        tc.tile_pool(name="held", bufs=1) as held,
+        tc.tile_pool(name="work", bufs=2) as work,
+        tc.tile_pool(name="small", bufs=4) as small,
+        tc.psum_pool(name="psum", bufs=2) as psum,
+    ):
+        offsets = held.tile([P, N // 16], U16, name="offsets")
+        nc.sync.dma_start(offsets[:], offs)
+
+        table = [held.tile([P, S], F32, name=f"table{cb}") for cb in range(CB)]
+        wpe_sb = held.tile([P, CB * N], F32, name="wpe_sb")
+        nc.sync.dma_start(table[0][:], wte[0:P, :])
+        nc.sync.dma_start(blocks(wpe_sb[:], CB), wpe.rearrange("(a p) j -> p a j", p=P))
+        for cb in range(1, CB):
+            nc.sync.dma_start(table[cb][:], wte[cb * P : (cb + 1) * P, :])
+
+        def load_weights(w, name):
+            w_sb = held.tile([P, CB * C], BF16, name=name)
+            nc.sync.dma_start(blocks(w_sb[:], CB), w.rearrange("(a p) m -> p a m", p=P))
+            return w_sb
+
+        wq_sb = load_weights(wq, "wq_sb")
+        wk_sb = load_weights(wk, "wk_sb")
+        wv_sb = load_weights(wv, "wv_sb")
+        wo_sb = load_weights(wo, "wo_sb")
+
+        def load_column(vec, name):
+            col = held.tile([P, CB], F32, name=name)
+            nc.scalar.dma_start(col[:], vec.rearrange("(a p) o -> p (a o)", p=P))
+            return col
+
+        with nc.allow_non_contiguous_dma(reason="one float32 to a partition, 512 in all"):
+            gain_col = load_column(ln_gain, "gain_col")
+            bias_col = load_column(ln_bias, "bias_col")
+            bq_col = load_column(bq, "bq_col")
+            bv_col = load_column(bv, "bv_col")
+            gate_col = load_column(gate, "gate_col")
+
+        ident_f = held.tile([P, P], F32, name="ident_f")
+        make_identity(nc, ident_f[:])
+        ident_b = held.tile([P, P], BF16, name="ident_b")
+        make_identity(nc, ident_b[:])
+        causal = held.tile([P, P], BF16, name="causal")
+        nc.gpsimd.memset(causal[:], 0.0)
+        nc.gpsimd.affine_select(
+            out=causal[:],
+            in_=causal[:],
+            pattern=[[-1, P]],
+            compare_op=ALU.is_ge,
+            fill=MASKED,
+            base=0,
+            channel_multiplier=1,
+        )
+        neg_half = held.tile([P, 1], F32, name="neg_half")
+        nc.gpsimd.memset(neg_half[:], -0.5)
+
+        bv_ps = psum.tile([P, C], F32, name="bv_ps", tag="lin")
+        for n in range(H):
+            bv_rep = work.tile([P, P], F32, name="bv_rep")
+            nc.vector.tensor_copy(out=bv_rep[:], in_=bv_col[:, n : n + 1].to_broadcast([P, P]))
+            nc.tensor.transpose(out=bv_ps[:, n * P : (n + 1) * P], in_=bv_rep[:], identity=ident_f[:])
+        bv_row = held.tile([P, C], F32, name="bv_row")
+        nc.vector.tensor_copy(out=bv_row[:], in_=bv_ps[:])
+
+        h_sb = held.tile([P, CB * N], F32, name="h_sb")
+        k_sb = held.tile([P, H * N], BF16, name="k_sb")
+        vT_sb = held.tile([P, JB * C], BF16, name="vT_sb")
+
+        for jb in range(JB):
+            tokens = slice(jb * P, (jb + 1) * P)
+            seen = (jb + 1) * P
+
+            for cb in range(CB):
+                nc.vector.tensor_tensor(
+                    out=h_sb[:, cb * N + jb * P : cb * N + (jb + 1) * P],
+                    in0=table[cb][:].indirect(offsets[:, jb * (P // 16) : (jb + 1) * (P // 16)]),
+                    in1=wpe_sb[:, cb * N + jb * P : cb * N + (jb + 1) * P],
+                    op=ALU.add,
+                )
+
+            hT_ps = psum.tile([P, C], F32, name="hT_ps", tag="lin")
+            for cb in range(CB):
+                nc.tensor.transpose(
+                    out=hT_ps[:, cb * P : (cb + 1) * P],
+                    in_=h_sb[:, cb * N + jb * P : cb * N + (jb + 1) * P],
+                    identity=ident_f[:],
+                )
+            stats = small.tile([P, 6], F32, name="stats")
+            nc.vector.bn_stats(out=stats[:], in_=hT_ps[:])
+            mean_var = small.tile([P, 2], F32, name="mean_var")
+            nc.vector.bn_aggr(out=mean_var[:], in_=stats[:])
+            var_eps = small.tile([P, 1], F32, name="var_eps")
+            nc.gpsimd.tensor_scalar(
+                out=var_eps[:], in0=mean_var[:, 1:2], scalar1=EPS, scalar2=None, op0=ALU.add
+            )
+            rstd = small.tile([P, 1], F32, name="rstd")
+            nc.gpsimd.tensor_tensor(out=rstd[:], in0=var_eps[:], in1=neg_half[:], op=ALU.pow)
+            normT = work.tile([P, C], F32, name="normT")
+            nc.vector.tensor_scalar(
+                out=normT[:],
+                in0=hT_ps[:],
+                scalar1=mean_var[:, 0:1],
+                scalar2=rstd[:],
+                op0=ALU.subtract,
+                op1=ALU.mult,
+            )
+            norm_ps = psum.tile([P, C], F32, name="norm_ps", tag="lin")
+            x_blk = work.tile([P, C], BF16, name="x_blk")
+            for cb in range(CB):
+                part = slice(cb * P, (cb + 1) * P)
+                nc.tensor.transpose(out=norm_ps[:, part], in_=normT[:, part], identity=ident_f[:])
+            for cb in range(CB):
+                part = slice(cb * P, (cb + 1) * P)
+                nc.scalar.activation(
+                    out=x_blk[:, part],
+                    in_=norm_ps[:, part],
+                    func=ACT.Identity,
+                    bias=bias_col[:, cb : cb + 1],
+                    scale=gain_col[:, cb : cb + 1],
+                )
+
+            q_ps = psum.tile([P, C], F32, name="q_ps", tag="lin")
+            for n in range(H):
+                for cb in range(CB):
+                    nc.tensor.matmul(
+                        q_ps[:, n * P : (n + 1) * P],
+                        lhsT=wq_sb[:, cb * C + n * P : cb * C + (n + 1) * P],
+                        rhs=x_blk[:, cb * P : (cb + 1) * P],
+                        start=(cb == 0),
+                        stop=(cb == CB - 1),
+                    )
+            q_blk = work.tile([P, C], BF16, name="q_blk")
+            nc.vector.tensor_tensor(
+                out=blocks(q_blk[:], H),
+                in0=blocks(q_ps[:], H),
+                in1=bq_col[:].unsqueeze(2).to_broadcast([P, H, P]),
+                op=ALU.add,
+            )
+            k_ps = psum.tile([P, C], F32, name="k_ps", tag="lin")
+            for n in range(H):
+                for cb in range(CB):
+                    nc.tensor.matmul(
+                        k_ps[:, n * P : (n + 1) * P],
+                        lhsT=wk_sb[:, cb * C + n * P : cb * C + (n + 1) * P],
+                        rhs=x_blk[:, cb * P : (cb + 1) * P],
+                        start=(cb == 0),
+                        stop=(cb == CB - 1),
+                    )
+            nc.scalar.copy(out=blocks(k_sb[:], H)[:, :, tokens], in_=blocks(k_ps[:], H))
+            v_ps = psum.tile([P, C], F32, name="v_ps", tag="lin")
+            for cb in range(CB):
+                nc.tensor.matmul(
+                    v_ps[:],
+                    lhsT=x_blk[:, cb * P : (cb + 1) * P],
+                    rhs=wv_sb[:, cb * C : (cb + 1) * C],
+                    start=(cb == 0),
+                    stop=(cb == CB - 1),
+                )
+            nc.vector.tensor_tensor(
+                out=vT_sb[:, jb * C : (jb + 1) * C], in0=v_ps[:], in1=bv_row[:], op=ALU.add
+            )
+
+            oT_ps = psum.tile([P, C], F32, name="oT_ps", tag="acc")
+            row_sum = small.tile([P, H], F32, name="row_sum")
+            for n in range(H):
+                q_head = q_blk[:, n * P : (n + 1) * P]
+                neg_s = work.tile([P, N], F32, name="neg_s", bufs=3)
+                neg_max = None
+                for lo in range(0, seen, BANK):
+                    hi = min(lo + BANK, seen)
+                    s_ps = psum.tile([P, BANK], F32, name="s_ps", tag="s")
+                    before_diag = min(hi, seen - P)
+                    if before_diag > lo:
+                        nc.tensor.matmul(
+                            s_ps[:, 0 : before_diag - lo],
+                            lhsT=q_head,
+                            rhs=k_sb[:, n * N + lo : n * N + before_diag],
+                            start=True,
+                            stop=True,
+                        )
+                    if hi == seen:
+                        diag = s_ps[:, seen - P - lo : seen - lo]
+                        nc.tensor.matmul(
+                            diag,
+                            lhsT=q_head,
+                            rhs=k_sb[:, n * N + seen - P : n * N + seen],
+                            start=True,
+                            stop=False,
+                        )
+                        nc.tensor.matmul(diag, lhsT=ident_b[:], rhs=causal[:], start=False, stop=True)
+                    smallest = small.tile([P, 1], F32, name="smallest")
+                    nc.vector.tensor_scalar(
+                        out=neg_s[:, lo:hi],
+                        in0=s_ps[:, 0 : hi - lo],
+                        scalar1=-SCORE_SCALE,
+                        scalar2=neg_max,
+                        op0=ALU.mult,
+                        op1=ALU.min,
+                        accum_out=smallest[:],
+                    )
+                    neg_max = smallest[:]
+
+                p_sb = work.tile([P, N], BF16, name="p_sb", bufs=3)
+                nc.scalar.activation(
+                    out=p_sb[:, 0:seen],
+                    in_=neg_s[:, 0:seen],
+                    func=ACT.Exp,
+                    bias=neg_max,
+                    scale=-1.0,
+                    accum_out=row_sum[:, n : n + 1],
+                )
+                pT_ps = psum.tile([P, N], BF16, name="pT_ps", tag="flip")
+                for ib in range(jb + 1):
+                    part = slice(ib * P, (ib + 1) * P)
+                    nc.tensor.transpose(out=pT_ps[:, part], in_=p_sb[:, part], identity=ident_b[:])
+                pT_sb = work.tile([P, N], BF16, name="pT_sb", bufs=3)
+                if n % 2 == 0:
+                    nc.scalar.copy(out=pT_sb[:, 0:seen], in_=pT_ps[:, 0:seen])
+                else:
+                    nc.vector.tensor_copy(out=pT_sb[:, 0:seen], in_=pT_ps[:, 0:seen])
+                for ib in range(jb + 1):
+                    nc.tensor.matmul(
+                        oT_ps[:, n * P : (n + 1) * P],
+                        lhsT=pT_sb[:, ib * P : (ib + 1) * P],
+                        rhs=vT_sb[:, ib * C + n * P : ib * C + (n + 1) * P],
+                        start=(ib == 0),
+                        stop=(ib == jb),
+                    )
+
+            inv_sum = small.tile([P, H], F32, name="inv_sum")
+            nc.vector.reciprocal(out=inv_sum[:], in_=row_sum[:])
+            head_scale = small.tile([P, H], F32, name="head_scale")
+            nc.vector.tensor_tensor(out=head_scale[:], in0=inv_sum[:], in1=gate_col[:], op=ALU.mult)
+            oT_sb = work.tile([P, C], BF16, name="oT_sb")
+            nc.vector.tensor_tensor(
+                out=blocks(oT_sb[:], H),
+                in0=blocks(oT_ps[:], H),
+                in1=head_scale[:].unsqueeze(2).to_broadcast([P, H, P]),
+                op=ALU.mult,
+            )
+            o_ps = psum.tile([P, C], BF16, name="o_ps", tag="flip")
+            for n in range(H):
+                part = slice(n * P, (n + 1) * P)
+                nc.tensor.transpose(out=o_ps[:, part], in_=oT_sb[:, part], identity=ident_b[:])
+            o_sb = work.tile([P, C], BF16, name="o_sb")
+            nc.scalar.copy(out=o_sb[:], in_=o_ps[:])
+
+            y_ps = psum.tile([P, C], F32, name="y_ps", tag="acc")
+            for cb in range(CB):
+                for n in range(H):
+                    nc.tensor.matmul(
+                        y_ps[:, cb * P : (cb + 1) * P],
+                        lhsT=wo_sb[:, n * C + cb * P : n * C + (cb + 1) * P],
+                        rhs=o_sb[:, n * P : (n + 1) * P],
+                        start=(n == 0),
+                        stop=(n == H - 1),
+                    )
+            y_sb = work.tile([P, C], F32, name="y_sb")
+            nc.vector.tensor_tensor(
+                out=blocks(y_sb[:], CB),
+                in0=blocks(y_ps[:], CB),
+                in1=blocks(h_sb[:], CB)[:, :, tokens],
+                op=ALU.add,
+            )
+            nc.sync.dma_start(
+                out.rearrange("(a p) j -> p a j", p=P)[:, :, tokens], blocks(y_sb[:], CB)
+            )

@@ -17,6 +17,8 @@ S = 4096
 N = 1024
 JB = N // P
 BANK = 512
+LEAD = 3
+EARLY = LEAD * P
 EPS = 1e-5
 SCORE_SCALE = 1.0 / math.sqrt(P)
 MASKED = -1.0e30
@@ -43,8 +45,9 @@ def tile_adaptivetransformermodel_b_kernel(
 
         table = [held.tile([P, S], F32, name=f"table{cb}") for cb in range(CB)]
         wpe_sb = held.tile([P, CB * N], F32, name="wpe_sb")
+        wpe_blocks = wpe.rearrange("(a p) j -> p a j", p=P)
         nc.sync.dma_start(table[0][:], wte[0:P, :])
-        nc.sync.dma_start(blocks(wpe_sb[:], CB), wpe.rearrange("(a p) j -> p a j", p=P))
+        nc.sync.dma_start(blocks(wpe_sb[:], CB)[:, :, 0:EARLY], wpe_blocks[:, :, 0:EARLY])
         for cb in range(1, CB):
             nc.sync.dma_start(table[cb][:], wte[cb * P : (cb + 1) * P, :])
 
@@ -56,19 +59,8 @@ def tile_adaptivetransformermodel_b_kernel(
         wq_sb = load_weights(wq, "wq_sb")
         wk_sb = load_weights(wk, "wk_sb")
         wv_sb = load_weights(wv, "wv_sb")
+        nc.sync.dma_start(blocks(wpe_sb[:], CB)[:, :, EARLY:N], wpe_blocks[:, :, EARLY:N])
         wo_sb = load_weights(wo, "wo_sb")
-
-        def load_column(vec, name):
-            col = held.tile([P, CB], F32, name=name)
-            nc.scalar.dma_start(col[:], vec.rearrange("(a p) o -> p (a o)", p=P))
-            return col
-
-        with nc.allow_non_contiguous_dma(reason="one float32 to a partition, 512 in all"):
-            gain_col = load_column(ln_gain, "gain_col")
-            bias_col = load_column(ln_bias, "bias_col")
-            bq_col = load_column(bq, "bq_col")
-            bv_col = load_column(bv, "bv_col")
-            gate_col = load_column(gate, "gate_col")
 
         ident_f = held.tile([P, P], F32, name="ident_f")
         make_identity(nc, ident_f[:])
@@ -88,7 +80,38 @@ def tile_adaptivetransformermodel_b_kernel(
         neg_half = held.tile([P, 1], F32, name="neg_half")
         nc.gpsimd.memset(neg_half[:], -0.5)
 
-        bv_ps = psum.tile([P, C], F32, name="bv_ps", tag="lin")
+        vector_rows = held.tile([P, P], F32, name="vector_rows")
+        nc.gpsimd.memset(vector_rows[:], 0.0)
+        for v, vec in enumerate((ln_gain, ln_bias, bq, bv, gate)):
+            nc.scalar.dma_start(
+                vector_rows[v * CB : (v + 1) * CB, :], vec.rearrange("(a p) o -> a (p o)", p=P)
+            )
+        columns_ps = psum.tile([P, P], F32, name="columns_ps", tag="mm", bufs=4)
+        nc.tensor.transpose(out=columns_ps[:], in_=vector_rows[:], identity=ident_f[:])
+        columns = held.tile([P, 5 * CB], F32, name="columns")
+        nc.vector.tensor_copy(out=columns[:], in_=columns_ps[:, 0 : 5 * CB])
+        gain_col = columns[:, 0 * CB : 1 * CB]
+        bias_col = columns[:, 1 * CB : 2 * CB]
+        bq_col = columns[:, 2 * CB : 3 * CB]
+        bv_col = columns[:, 3 * CB : 4 * CB]
+        gate_col = columns[:, 4 * CB : 5 * CB]
+
+        h_sb = held.tile([P, CB * N], F32, name="h_sb")
+        k_sb = held.tile([P, H * N], BF16, name="k_sb")
+        vT_sb = held.tile([P, JB * C], BF16, name="vT_sb")
+
+        def look_up(cb, first, count):
+            nc.vector.tensor_tensor(
+                out=h_sb[:, cb * N + first : cb * N + first + count],
+                in0=table[cb][:].indirect(offsets[:, first // 16 : (first + count) // 16]),
+                in1=wpe_sb[:, cb * N + first : cb * N + first + count],
+                op=ALU.add,
+            )
+
+        for cb in range(CB - 1):
+            look_up(cb, 0, EARLY)
+
+        bv_ps = psum.tile([P, C], F32, name="bv_ps", tag="mm", bufs=4)
         for n in range(H):
             bv_rep = work.tile([P, P], F32, name="bv_rep")
             nc.vector.tensor_copy(out=bv_rep[:], in_=bv_col[:, n : n + 1].to_broadcast([P, P]))
@@ -96,206 +119,278 @@ def tile_adaptivetransformermodel_b_kernel(
         bv_row = held.tile([P, C], F32, name="bv_row")
         nc.vector.tensor_copy(out=bv_row[:], in_=bv_ps[:])
 
-        h_sb = held.tile([P, CB * N], F32, name="h_sb")
-        k_sb = held.tile([P, H * N], BF16, name="k_sb")
-        vT_sb = held.tile([P, JB * C], BF16, name="vT_sb")
+        hT_ps, mean_var, rstd, shift, normT, x_blk, q_blk = {}, {}, {}, {}, {}, {}, {}
+        neg_s, neg_max, p_sb, pT_sb = {}, {}, {}, {}
+        row_sum, oT_ps, oT_sb, o_sb, y_ps = {}, {}, {}, {}, {}
 
-        for jb in range(JB):
-            tokens = slice(jb * P, (jb + 1) * P)
-            seen = (jb + 1) * P
-
+        def look_up_block(b):
             for cb in range(CB):
-                nc.vector.tensor_tensor(
-                    out=h_sb[:, cb * N + jb * P : cb * N + (jb + 1) * P],
-                    in0=table[cb][:].indirect(offsets[:, jb * (P // 16) : (jb + 1) * (P // 16)]),
-                    in1=wpe_sb[:, cb * N + jb * P : cb * N + (jb + 1) * P],
-                    op=ALU.add,
-                )
+                if cb == CB - 1 or b * P >= EARLY:
+                    look_up(cb, b * P, P)
 
-            hT_ps = psum.tile([P, C], F32, name="hT_ps", tag="lin")
+        def token_statistics(b):
+            hT_ps[b] = psum.tile([P, C], F32, name="hT_ps", tag="mm", bufs=4)
             for cb in range(CB):
                 nc.tensor.transpose(
-                    out=hT_ps[:, cb * P : (cb + 1) * P],
-                    in_=h_sb[:, cb * N + jb * P : cb * N + (jb + 1) * P],
+                    out=hT_ps[b][:, cb * P : (cb + 1) * P],
+                    in_=h_sb[:, cb * N + b * P : cb * N + (b + 1) * P],
                     identity=ident_f[:],
                 )
             stats = small.tile([P, 6], F32, name="stats")
-            nc.vector.bn_stats(out=stats[:], in_=hT_ps[:])
-            mean_var = small.tile([P, 2], F32, name="mean_var")
-            nc.vector.bn_aggr(out=mean_var[:], in_=stats[:])
+            nc.vector.bn_stats(out=stats[:], in_=hT_ps[b][:])
+            mean_var[b] = small.tile([P, 2], F32, name="mean_var")
+            nc.vector.bn_aggr(out=mean_var[b][:], in_=stats[:])
             var_eps = small.tile([P, 1], F32, name="var_eps")
             nc.gpsimd.tensor_scalar(
-                out=var_eps[:], in0=mean_var[:, 1:2], scalar1=EPS, scalar2=None, op0=ALU.add
+                out=var_eps[:], in0=mean_var[b][:, 1:2], scalar1=EPS, scalar2=None, op0=ALU.add
             )
-            rstd = small.tile([P, 1], F32, name="rstd")
-            nc.gpsimd.tensor_tensor(out=rstd[:], in0=var_eps[:], in1=neg_half[:], op=ALU.pow)
-            normT = work.tile([P, C], F32, name="normT")
-            nc.vector.tensor_scalar(
-                out=normT[:],
-                in0=hT_ps[:],
-                scalar1=mean_var[:, 0:1],
-                scalar2=rstd[:],
-                op0=ALU.subtract,
+            rstd[b] = small.tile([P, 1], F32, name="rstd")
+            nc.gpsimd.tensor_tensor(out=rstd[b][:], in0=var_eps[:], in1=neg_half[:], op=ALU.pow)
+            shift[b] = small.tile([P, 1], F32, name="shift")
+            nc.gpsimd.tensor_scalar(
+                out=shift[b][:],
+                in0=mean_var[b][:, 0:1],
+                scalar1=rstd[b][:],
+                scalar2=-1.0,
+                op0=ALU.mult,
                 op1=ALU.mult,
             )
-            norm_ps = psum.tile([P, C], F32, name="norm_ps", tag="lin")
-            x_blk = work.tile([P, C], BF16, name="x_blk")
+
+        def normalise(b):
+            normT[b] = work.tile([P, C], F32, name="normT", bufs=LEAD)
+            nc.scalar.activation(
+                out=normT[b][:],
+                in_=hT_ps[b][:],
+                func=ACT.Identity,
+                bias=shift[b][:],
+                scale=rstd[b][:],
+            )
+
+        def gain_and_bias(b):
+            norm_ps = psum.tile([P, C], F32, name="norm_ps", tag="mm", bufs=4)
+            x_blk[b] = work.tile([P, C], BF16, name="x_blk", bufs=LEAD)
             for cb in range(CB):
                 part = slice(cb * P, (cb + 1) * P)
-                nc.tensor.transpose(out=norm_ps[:, part], in_=normT[:, part], identity=ident_f[:])
+                nc.tensor.transpose(out=norm_ps[:, part], in_=normT[b][:, part], identity=ident_f[:])
             for cb in range(CB):
                 part = slice(cb * P, (cb + 1) * P)
                 nc.scalar.activation(
-                    out=x_blk[:, part],
+                    out=x_blk[b][:, part],
                     in_=norm_ps[:, part],
                     func=ACT.Identity,
                     bias=bias_col[:, cb : cb + 1],
                     scale=gain_col[:, cb : cb + 1],
                 )
 
-            q_ps = psum.tile([P, C], F32, name="q_ps", tag="lin")
+        def project_heads(w_sb, b, name):
+            ps = psum.tile([P, C], F32, name=name, tag="mm", bufs=4)
             for n in range(H):
                 for cb in range(CB):
                     nc.tensor.matmul(
-                        q_ps[:, n * P : (n + 1) * P],
-                        lhsT=wq_sb[:, cb * C + n * P : cb * C + (n + 1) * P],
-                        rhs=x_blk[:, cb * P : (cb + 1) * P],
+                        ps[:, n * P : (n + 1) * P],
+                        lhsT=w_sb[:, cb * C + n * P : cb * C + (n + 1) * P],
+                        rhs=x_blk[b][:, cb * P : (cb + 1) * P],
                         start=(cb == 0),
                         stop=(cb == CB - 1),
                     )
-            q_blk = work.tile([P, C], BF16, name="q_blk")
-            nc.vector.tensor_tensor(
-                out=blocks(q_blk[:], H),
-                in0=blocks(q_ps[:], H),
-                in1=bq_col[:].unsqueeze(2).to_broadcast([P, H, P]),
-                op=ALU.add,
-            )
-            k_ps = psum.tile([P, C], F32, name="k_ps", tag="lin")
+            return ps
+
+        def project_q(b):
+            q_ps = project_heads(wq_sb, b, "q_ps")
+            q_blk[b] = work.tile([P, C], BF16, name="q_blk")
             for n in range(H):
-                for cb in range(CB):
-                    nc.tensor.matmul(
-                        k_ps[:, n * P : (n + 1) * P],
-                        lhsT=wk_sb[:, cb * C + n * P : cb * C + (n + 1) * P],
-                        rhs=x_blk[:, cb * P : (cb + 1) * P],
-                        start=(cb == 0),
-                        stop=(cb == CB - 1),
-                    )
-            nc.scalar.copy(out=blocks(k_sb[:], H)[:, :, tokens], in_=blocks(k_ps[:], H))
-            v_ps = psum.tile([P, C], F32, name="v_ps", tag="lin")
+                part = slice(n * P, (n + 1) * P)
+                nc.scalar.activation(
+                    out=q_blk[b][:, part], in_=q_ps[:, part], func=ACT.Identity, bias=bq_col[:, n : n + 1]
+                )
+
+        def project_k(b):
+            k_ps = project_heads(wk_sb, b, "k_ps")
+            nc.scalar.copy(out=blocks(k_sb[:], H)[:, :, b * P : (b + 1) * P], in_=blocks(k_ps[:], H))
+
+        def project_v(b):
+            v_ps = psum.tile([P, C], F32, name="v_ps", tag="mm", bufs=4)
             for cb in range(CB):
                 nc.tensor.matmul(
                     v_ps[:],
-                    lhsT=x_blk[:, cb * P : (cb + 1) * P],
+                    lhsT=x_blk[b][:, cb * P : (cb + 1) * P],
                     rhs=wv_sb[:, cb * C : (cb + 1) * C],
                     start=(cb == 0),
                     stop=(cb == CB - 1),
                 )
             nc.vector.tensor_tensor(
-                out=vT_sb[:, jb * C : (jb + 1) * C], in0=v_ps[:], in1=bv_row[:], op=ALU.add
+                out=vT_sb[:, b * C : (b + 1) * C], in0=v_ps[:], in1=bv_row[:], op=ALU.add
             )
 
-            oT_ps = psum.tile([P, C], F32, name="oT_ps", tag="acc")
-            row_sum = small.tile([P, H], F32, name="row_sum")
-            for n in range(H):
-                q_head = q_blk[:, n * P : (n + 1) * P]
-                neg_s = work.tile([P, N], F32, name="neg_s", bufs=3)
-                neg_max = None
-                for lo in range(0, seen, BANK):
-                    hi = min(lo + BANK, seen)
-                    s_ps = psum.tile([P, BANK], F32, name="s_ps", tag="s")
-                    before_diag = min(hi, seen - P)
-                    if before_diag > lo:
-                        nc.tensor.matmul(
-                            s_ps[:, 0 : before_diag - lo],
-                            lhsT=q_head,
-                            rhs=k_sb[:, n * N + lo : n * N + before_diag],
-                            start=True,
-                            stop=True,
-                        )
-                    if hi == seen:
-                        diag = s_ps[:, seen - P - lo : seen - lo]
-                        nc.tensor.matmul(
-                            diag,
-                            lhsT=q_head,
-                            rhs=k_sb[:, n * N + seen - P : n * N + seen],
-                            start=True,
-                            stop=False,
-                        )
-                        nc.tensor.matmul(diag, lhsT=ident_b[:], rhs=causal[:], start=False, stop=True)
-                    smallest = small.tile([P, 1], F32, name="smallest")
-                    nc.vector.tensor_scalar(
-                        out=neg_s[:, lo:hi],
-                        in0=s_ps[:, 0 : hi - lo],
-                        scalar1=-SCORE_SCALE,
-                        scalar2=neg_max,
-                        op0=ALU.mult,
-                        op1=ALU.min,
-                        accum_out=smallest[:],
-                    )
-                    neg_max = smallest[:]
-
-                p_sb = work.tile([P, N], BF16, name="p_sb", bufs=3)
-                nc.scalar.activation(
-                    out=p_sb[:, 0:seen],
-                    in_=neg_s[:, 0:seen],
-                    func=ACT.Exp,
-                    bias=neg_max,
-                    scale=-1.0,
-                    accum_out=row_sum[:, n : n + 1],
-                )
-                pT_ps = psum.tile([P, N], BF16, name="pT_ps", tag="flip")
-                for ib in range(jb + 1):
-                    part = slice(ib * P, (ib + 1) * P)
-                    nc.tensor.transpose(out=pT_ps[:, part], in_=p_sb[:, part], identity=ident_b[:])
-                pT_sb = work.tile([P, N], BF16, name="pT_sb", bufs=3)
-                if n % 2 == 0:
-                    nc.scalar.copy(out=pT_sb[:, 0:seen], in_=pT_ps[:, 0:seen])
-                else:
-                    nc.vector.tensor_copy(out=pT_sb[:, 0:seen], in_=pT_ps[:, 0:seen])
-                for ib in range(jb + 1):
+        def scores(b, n):
+            seen = (b + 1) * P
+            q_head = q_blk[b][:, n * P : (n + 1) * P]
+            neg_s[b, n] = work.tile([P, N], F32, name="neg_s", bufs=3)
+            neg_max[b, n] = None
+            for lo in range(0, seen, BANK):
+                hi = min(lo + BANK, seen)
+                s_ps = psum.tile([P, BANK], F32, name="s_ps", tag="mm", bufs=4)
+                before_diag = min(hi, seen - P)
+                if before_diag > lo:
                     nc.tensor.matmul(
-                        oT_ps[:, n * P : (n + 1) * P],
-                        lhsT=pT_sb[:, ib * P : (ib + 1) * P],
-                        rhs=vT_sb[:, ib * C + n * P : ib * C + (n + 1) * P],
-                        start=(ib == 0),
-                        stop=(ib == jb),
+                        s_ps[:, 0 : before_diag - lo],
+                        lhsT=q_head,
+                        rhs=k_sb[:, n * N + lo : n * N + before_diag],
+                        start=True,
+                        stop=True,
                     )
+                if hi == seen:
+                    diag = s_ps[:, seen - P - lo : seen - lo]
+                    nc.tensor.matmul(
+                        diag,
+                        lhsT=q_head,
+                        rhs=k_sb[:, n * N + seen - P : n * N + seen],
+                        start=True,
+                        stop=False,
+                    )
+                    nc.tensor.matmul(diag, lhsT=ident_b[:], rhs=causal[:], start=False, stop=True)
+                smallest = small.tile([P, 1], F32, name="smallest", bufs=8)
+                nc.vector.tensor_scalar(
+                    out=neg_s[b, n][:, lo:hi],
+                    in0=s_ps[:, 0 : hi - lo],
+                    scalar1=-SCORE_SCALE,
+                    scalar2=neg_max[b, n],
+                    op0=ALU.mult,
+                    op1=ALU.min,
+                    accum_out=smallest[:],
+                )
+                neg_max[b, n] = smallest[:]
 
-            inv_sum = small.tile([P, H], F32, name="inv_sum")
-            nc.vector.reciprocal(out=inv_sum[:], in_=row_sum[:])
-            head_scale = small.tile([P, H], F32, name="head_scale")
-            nc.vector.tensor_tensor(out=head_scale[:], in0=inv_sum[:], in1=gate_col[:], op=ALU.mult)
-            oT_sb = work.tile([P, C], BF16, name="oT_sb")
-            nc.vector.tensor_tensor(
-                out=blocks(oT_sb[:], H),
-                in0=blocks(oT_ps[:], H),
-                in1=head_scale[:].unsqueeze(2).to_broadcast([P, H, P]),
-                op=ALU.mult,
+        def exponentials(b, n):
+            seen = (b + 1) * P
+            if n == 0:
+                row_sum[b] = small.tile([P, H], F32, name="row_sum")
+            p_sb[b, n] = work.tile([P, N], BF16, name="p_sb", bufs=4)
+            nc.scalar.activation(
+                out=p_sb[b, n][:, 0:seen],
+                in_=neg_s[b, n][:, 0:seen],
+                func=ACT.Exp,
+                bias=neg_max[b, n],
+                scale=-1.0,
+                accum_out=row_sum[b][:, n : n + 1],
             )
+
+        def keys_to_partitions(b, n):
+            seen = (b + 1) * P
+            pT_ps = psum.tile([P, N], BF16, name="pT_ps", tag="flip")
+            for ib in range(b + 1):
+                part = slice(ib * P, (ib + 1) * P)
+                nc.tensor.transpose(out=pT_ps[:, part], in_=p_sb[b, n][:, part], identity=ident_b[:])
+            pT_sb[b, n] = work.tile([P, N], BF16, name="pT_sb", bufs=3)
+            if n == 0:
+                nc.scalar.copy(out=pT_sb[b, n][:, 0:seen], in_=pT_ps[:, 0:seen])
+            else:
+                nc.vector.tensor_copy(out=pT_sb[b, n][:, 0:seen], in_=pT_ps[:, 0:seen])
+
+        def weighted_sum(b, n):
+            if n == 0:
+                oT_ps[b] = psum.tile([P, C], F32, name="oT_ps", tag="acc")
+            for ib in range(b + 1):
+                nc.tensor.matmul(
+                    oT_ps[b][:, n * P : (n + 1) * P],
+                    lhsT=pT_sb[b, n][:, ib * P : (ib + 1) * P],
+                    rhs=vT_sb[:, ib * C + n * P : ib * C + (n + 1) * P],
+                    start=(ib == 0),
+                    stop=(ib == b),
+                )
+
+        def divide_and_gate(b):
+            inv_sum = small.tile([P, H], F32, name="inv_sum")
+            nc.vector.reciprocal(out=inv_sum[:], in_=row_sum[b][:])
+            head_scale = small.tile([P, H], F32, name="head_scale")
+            nc.vector.tensor_tensor(out=head_scale[:], in0=inv_sum[:], in1=gate_col, op=ALU.mult)
+            oT_sb[b] = work.tile([P, C], BF16, name="oT_sb")
+            for n in range(H):
+                part = slice(n * P, (n + 1) * P)
+                nc.scalar.activation(
+                    out=oT_sb[b][:, part],
+                    in_=oT_ps[b][:, part],
+                    func=ACT.Identity,
+                    scale=head_scale[:, n : n + 1],
+                )
+
+        def channels_to_partitions(b):
             o_ps = psum.tile([P, C], BF16, name="o_ps", tag="flip")
             for n in range(H):
                 part = slice(n * P, (n + 1) * P)
-                nc.tensor.transpose(out=o_ps[:, part], in_=oT_sb[:, part], identity=ident_b[:])
-            o_sb = work.tile([P, C], BF16, name="o_sb")
-            nc.scalar.copy(out=o_sb[:], in_=o_ps[:])
+                nc.tensor.transpose(out=o_ps[:, part], in_=oT_sb[b][:, part], identity=ident_b[:])
+            o_sb[b] = work.tile([P, C], BF16, name="o_sb")
+            nc.vector.tensor_copy(out=o_sb[b][:], in_=o_ps[:])
 
-            y_ps = psum.tile([P, C], F32, name="y_ps", tag="acc")
+        def project_out(b):
+            y_ps[b] = psum.tile([P, C], F32, name="y_ps", tag="acc")
             for cb in range(CB):
                 for n in range(H):
                     nc.tensor.matmul(
-                        y_ps[:, cb * P : (cb + 1) * P],
+                        y_ps[b][:, cb * P : (cb + 1) * P],
                         lhsT=wo_sb[:, n * C + cb * P : n * C + (cb + 1) * P],
-                        rhs=o_sb[:, n * P : (n + 1) * P],
+                        rhs=o_sb[b][:, n * P : (n + 1) * P],
                         start=(n == 0),
                         stop=(n == H - 1),
                     )
+
+        def residual_and_store(b):
+            tokens = slice(b * P, (b + 1) * P)
             y_sb = work.tile([P, C], F32, name="y_sb")
             nc.vector.tensor_tensor(
                 out=blocks(y_sb[:], CB),
-                in0=blocks(y_ps[:], CB),
+                in0=blocks(y_ps[b][:], CB),
                 in1=blocks(h_sb[:], CB)[:, :, tokens],
                 op=ALU.add,
             )
             nc.sync.dma_start(
                 out.rearrange("(a p) j -> p a j", p=P)[:, :, tokens], blocks(y_sb[:], CB)
             )
+
+        def block_head(step):
+            return divmod(step, H) if 0 <= step < JB * H else None
+
+        def layer_norm_part(b, part):
+            if part == 0:
+                look_up_block(b)
+            if part == 1:
+                token_statistics(b)
+            if part == 2:
+                normalise(b)
+            if part == 3:
+                gain_and_bias(b)
+
+        for part in range(4):
+            for b in range(LEAD):
+                layer_norm_part(b, part)
+
+        END_LAG = 7
+        for step in range(-H, JB * H + END_LAG):
+            b, n = divmod(step, H)
+            if block_head(step):
+                scores(b, n)
+            if LEAD <= b + LEAD < JB:
+                layer_norm_part(b + LEAD, n)
+            if 0 <= b + 1 < JB:
+                if n == 0:
+                    project_q(b + 1)
+                if n == 1:
+                    project_k(b + 1)
+                if n == 2:
+                    project_v(b + 1)
+            if block_head(step):
+                exponentials(b, n)
+            if block_head(step - 2):
+                keys_to_partitions(*block_head(step - 2))
+            if block_head(step - END_LAG):
+                ended, part = block_head(step - END_LAG)
+                if part == 0:
+                    divide_and_gate(ended)
+                if part == 1:
+                    channels_to_partitions(ended)
+                if part == 2:
+                    project_out(ended)
+                if part == 3:
+                    residual_and_store(ended)
+            if block_head(step - 3):
+                weighted_sum(*block_head(step - 3))

@@ -120,7 +120,7 @@ def tile_adaptivetransformermodel_b_kernel(
         nc.vector.tensor_copy(out=bv_row[:], in_=bv_ps[:])
 
         hT_ps, mean_var, rstd, shift, normT, x_blk, q_blk = {}, {}, {}, {}, {}, {}, {}
-        neg_s, neg_max, p_sb, pT_sb = {}, {}, {}, {}
+        s_banks, neg_s, neg_max, p_sb, pT_sb = {}, {}, {}, {}, {}
         row_sum, oT_ps, oT_sb, o_sb, y_ps = {}, {}, {}, {}, {}
 
         def look_up_block(b):
@@ -227,9 +227,11 @@ def tile_adaptivetransformermodel_b_kernel(
             q_head = q_blk[b][:, n * P : (n + 1) * P]
             neg_s[b, n] = work.tile([P, N], F32, name="neg_s", bufs=3)
             neg_max[b, n] = None
+            s_banks[b, n] = []
             for lo in range(0, seen, BANK):
                 hi = min(lo + BANK, seen)
                 s_ps = psum.tile([P, BANK], F32, name="s_ps", tag="mm", bufs=4)
+                s_banks[b, n].append((lo, hi, s_ps))
                 before_diag = min(hi, seen - P)
                 if before_diag > lo:
                     nc.tensor.matmul(
@@ -249,6 +251,10 @@ def tile_adaptivetransformermodel_b_kernel(
                         stop=False,
                     )
                     nc.tensor.matmul(diag, lhsT=ident_b[:], rhs=causal[:], start=False, stop=True)
+
+        def move_scores(b, n, bank):
+            if bank < len(s_banks[b, n]):
+                lo, hi, s_ps = s_banks[b, n][bank]
                 smallest = small.tile([P, 1], F32, name="smallest", bufs=8)
                 nc.vector.tensor_scalar(
                     out=neg_s[b, n][:, lo:hi],
@@ -282,10 +288,7 @@ def tile_adaptivetransformermodel_b_kernel(
                 part = slice(ib * P, (ib + 1) * P)
                 nc.tensor.transpose(out=pT_ps[:, part], in_=p_sb[b, n][:, part], identity=ident_b[:])
             pT_sb[b, n] = work.tile([P, N], BF16, name="pT_sb", bufs=3)
-            if n == 0:
-                nc.scalar.copy(out=pT_sb[b, n][:, 0:seen], in_=pT_ps[:, 0:seen])
-            else:
-                nc.vector.tensor_copy(out=pT_sb[b, n][:, 0:seen], in_=pT_ps[:, 0:seen])
+            nc.vector.tensor_copy(out=pT_sb[b, n][:, 0:seen], in_=pT_ps[:, 0:seen])
 
         def weighted_sum(b, n):
             if n == 0:
@@ -369,6 +372,11 @@ def tile_adaptivetransformermodel_b_kernel(
             b, n = divmod(step, H)
             if block_head(step):
                 scores(b, n)
+                move_scores(b, n, 0)
+            if block_head(step - 2):
+                keys_to_partitions(*block_head(step - 2))
+            if block_head(step):
+                move_scores(b, n, 1)
             if LEAD <= b + LEAD < JB:
                 layer_norm_part(b + LEAD, n)
             if 0 <= b + 1 < JB:
@@ -380,8 +388,6 @@ def tile_adaptivetransformermodel_b_kernel(
                     project_v(b + 1)
             if block_head(step):
                 exponentials(b, n)
-            if block_head(step - 2):
-                keys_to_partitions(*block_head(step - 2))
             if block_head(step - END_LAG):
                 ended, part = block_head(step - END_LAG)
                 if part == 0:

@@ -288,7 +288,10 @@ def tile_adaptivetransformermodel_b_kernel(
                 part = slice(ib * P, (ib + 1) * P)
                 nc.tensor.transpose(out=pT_ps[:, part], in_=p_sb[b, n][:, part], identity=ident_b[:])
             pT_sb[b, n] = work.tile([P, N], BF16, name="pT_sb", bufs=3)
-            nc.vector.tensor_copy(out=pT_sb[b, n][:, 0:seen], in_=pT_ps[:, 0:seen])
+            if n % 2 == 0:
+                nc.scalar.copy(out=pT_sb[b, n][:, 0:seen], in_=pT_ps[:, 0:seen])
+            else:
+                nc.vector.tensor_copy(out=pT_sb[b, n][:, 0:seen], in_=pT_ps[:, 0:seen])
 
         def weighted_sum(b, n):
             if n == 0:

import math

import concourse.mybir as mybir
from concourse.masks import make_identity

F32 = mybir.dt.float32
BF16 = mybir.dt.bfloat16
U16 = mybir.dt.uint16
ALU = mybir.AluOpType
ACT = mybir.ActivationFunctionType

P = 128
C = 512
CB = C // P
H = 4
S = 4096
N = 1024
JB = N // P
BANK = 512
LEAD = 3
EARLY = LEAD * P
EPS = 1e-5
SCORE_SCALE = 1.0 / math.sqrt(P)
MASKED = -1.0e30

FLOPS = 4 * 2 * C * C * N + 2 * 2 * P * H * (N * (N + 1) // 2)


def blocks(ap, n):
    return ap.rearrange("p (a f) -> p a f", a=n)


def tile_adaptivetransformermodel_b_kernel(
    tc, wte, wpe, ln_gain, ln_bias, wq, bq, wk, wv, bv, wo, gate, offs, out
):
    nc = tc.nc
    with (
        tc.tile_pool(name="held", bufs=1) as held,
        tc.tile_pool(name="work", bufs=2) as work,
        tc.tile_pool(name="small", bufs=4) as small,
        tc.psum_pool(name="psum", bufs=2) as psum,
    ):
        offsets = held.tile([P, N // 16], U16, name="offsets")
        nc.sync.dma_start(offsets[:], offs)

        table = [held.tile([P, S], F32, name=f"table{cb}") for cb in range(CB)]
        wpe_sb = held.tile([P, CB * N], F32, name="wpe_sb")
        wpe_blocks = wpe.rearrange("(a p) j -> p a j", p=P)
        nc.sync.dma_start(table[0][:], wte[0:P, :])
        nc.sync.dma_start(blocks(wpe_sb[:], CB)[:, :, 0:EARLY], wpe_blocks[:, :, 0:EARLY])
        for cb in range(1, CB):
            nc.sync.dma_start(table[cb][:], wte[cb * P : (cb + 1) * P, :])

        def load_weights(w, name):
            w_sb = held.tile([P, CB * C], BF16, name=name)
            nc.sync.dma_start(blocks(w_sb[:], CB), w.rearrange("(a p) m -> p a m", p=P))
            return w_sb

        wq_sb = load_weights(wq, "wq_sb")
        wk_sb = load_weights(wk, "wk_sb")
        wv_sb = load_weights(wv, "wv_sb")
        nc.sync.dma_start(blocks(wpe_sb[:], CB)[:, :, EARLY:N], wpe_blocks[:, :, EARLY:N])
        wo_sb = load_weights(wo, "wo_sb")

        ident_f = held.tile([P, P], F32, name="ident_f")
        make_identity(nc, ident_f[:])
        ident_b = held.tile([P, P], BF16, name="ident_b")
        make_identity(nc, ident_b[:])
        causal = held.tile([P, P], BF16, name="causal")
        nc.gpsimd.memset(causal[:], 0.0)
        nc.gpsimd.affine_select(
            out=causal[:],
            in_=causal[:],
            pattern=[[-1, P]],
            compare_op=ALU.is_ge,
            fill=MASKED,
            base=0,
            channel_multiplier=1,
        )
        neg_half = held.tile([P, 1], F32, name="neg_half")
        nc.gpsimd.memset(neg_half[:], -0.5)

        vector_rows = held.tile([P, P], F32, name="vector_rows")
        nc.gpsimd.memset(vector_rows[:], 0.0)
        for v, vec in enumerate((ln_gain, ln_bias, bq, bv, gate)):
            nc.scalar.dma_start(
                vector_rows[v * CB : (v + 1) * CB, :], vec.rearrange("(a p) o -> a (p o)", p=P)
            )
        columns_ps = psum.tile([P, P], F32, name="columns_ps", tag="mm", bufs=4)
        nc.tensor.transpose(out=columns_ps[:], in_=vector_rows[:], identity=ident_f[:])
        columns = held.tile([P, 5 * CB], F32, name="columns")
        nc.vector.tensor_copy(out=columns[:], in_=columns_ps[:, 0 : 5 * CB])
        gain_col = columns[:, 0 * CB : 1 * CB]
        bias_col = columns[:, 1 * CB : 2 * CB]
        bq_col = columns[:, 2 * CB : 3 * CB]
        bv_col = columns[:, 3 * CB : 4 * CB]
        gate_col = columns[:, 4 * CB : 5 * CB]

        h_sb = held.tile([P, CB * N], F32, name="h_sb")
        k_sb = held.tile([P, H * N], BF16, name="k_sb")
        vT_sb = held.tile([P, JB * C], BF16, name="vT_sb")

        def look_up(cb, first, count):
            nc.vector.tensor_tensor(
                out=h_sb[:, cb * N + first : cb * N + first + count],
                in0=table[cb][:].indirect(offsets[:, first // 16 : (first + count) // 16]),
                in1=wpe_sb[:, cb * N + first : cb * N + first + count],
                op=ALU.add,
            )

        for cb in range(CB - 1):
            look_up(cb, 0, EARLY)

        bv_ps = psum.tile([P, C], F32, name="bv_ps", tag="mm", bufs=4)
        for n in range(H):
            bv_rep = work.tile([P, P], F32, name="bv_rep")
            nc.vector.tensor_copy(out=bv_rep[:], in_=bv_col[:, n : n + 1].to_broadcast([P, P]))
            nc.tensor.transpose(out=bv_ps[:, n * P : (n + 1) * P], in_=bv_rep[:], identity=ident_f[:])
        bv_row = held.tile([P, C], F32, name="bv_row")
        nc.vector.tensor_copy(out=bv_row[:], in_=bv_ps[:])

        hT_ps, mean_var, rstd, shift, normT, x_blk, q_blk = {}, {}, {}, {}, {}, {}, {}
        s_banks, neg_s, neg_max, p_sb, pT_sb = {}, {}, {}, {}, {}
        row_sum, oT_ps, oT_sb, o_sb, y_ps = {}, {}, {}, {}, {}

        def look_up_block(b):
            for cb in range(CB):
                if cb == CB - 1 or b * P >= EARLY:
                    look_up(cb, b * P, P)

        def token_statistics(b):
            hT_ps[b] = psum.tile([P, C], F32, name="hT_ps", tag="mm", bufs=4)
            for cb in range(CB):
                nc.tensor.transpose(
                    out=hT_ps[b][:, cb * P : (cb + 1) * P],
                    in_=h_sb[:, cb * N + b * P : cb * N + (b + 1) * P],
                    identity=ident_f[:],
                )
            stats = small.tile([P, 6], F32, name="stats")
            nc.vector.bn_stats(out=stats[:], in_=hT_ps[b][:])
            mean_var[b] = small.tile([P, 2], F32, name="mean_var")
            nc.vector.bn_aggr(out=mean_var[b][:], in_=stats[:])
            var_eps = small.tile([P, 1], F32, name="var_eps")
            nc.gpsimd.tensor_scalar(
                out=var_eps[:], in0=mean_var[b][:, 1:2], scalar1=EPS, scalar2=None, op0=ALU.add
            )
            rstd[b] = small.tile([P, 1], F32, name="rstd")
            nc.gpsimd.tensor_tensor(out=rstd[b][:], in0=var_eps[:], in1=neg_half[:], op=ALU.pow)
            shift[b] = small.tile([P, 1], F32, name="shift")
            nc.gpsimd.tensor_scalar(
                out=shift[b][:],
                in0=mean_var[b][:, 0:1],
                scalar1=rstd[b][:],
                scalar2=-1.0,
                op0=ALU.mult,
                op1=ALU.mult,
            )

        def normalise(b):
            normT[b] = work.tile([P, C], F32, name="normT", bufs=LEAD)
            nc.scalar.activation(
                out=normT[b][:],
                in_=hT_ps[b][:],
                func=ACT.Identity,
                bias=shift[b][:],
                scale=rstd[b][:],
            )

        def gain_and_bias(b):
            norm_ps = psum.tile([P, C], F32, name="norm_ps", tag="mm", bufs=4)
            x_blk[b] = work.tile([P, C], BF16, name="x_blk", bufs=LEAD)
            for cb in range(CB):
                part = slice(cb * P, (cb + 1) * P)
                nc.tensor.transpose(out=norm_ps[:, part], in_=normT[b][:, part], identity=ident_f[:])
            for cb in range(CB):
                part = slice(cb * P, (cb + 1) * P)
                nc.scalar.activation(
                    out=x_blk[b][:, part],
                    in_=norm_ps[:, part],
                    func=ACT.Identity,
                    bias=bias_col[:, cb : cb + 1],
                    scale=gain_col[:, cb : cb + 1],
                )

        def project_heads(w_sb, b, name):
            ps = psum.tile([P, C], F32, name=name, tag="mm", bufs=4)
            for n in range(H):
                for cb in range(CB):
                    nc.tensor.matmul(
                        ps[:, n * P : (n + 1) * P],
                        lhsT=w_sb[:, cb * C + n * P : cb * C + (n + 1) * P],
                        rhs=x_blk[b][:, cb * P : (cb + 1) * P],
                        start=(cb == 0),
                        stop=(cb == CB - 1),
                    )
            return ps

        def project_q(b):
            q_ps = project_heads(wq_sb, b, "q_ps")
            q_blk[b] = work.tile([P, C], BF16, name="q_blk")
            for n in range(H):
                part = slice(n * P, (n + 1) * P)
                nc.scalar.activation(
                    out=q_blk[b][:, part], in_=q_ps[:, part], func=ACT.Identity, bias=bq_col[:, n : n + 1]
                )

        def project_k(b):
            k_ps = project_heads(wk_sb, b, "k_ps")
            nc.scalar.copy(out=blocks(k_sb[:], H)[:, :, b * P : (b + 1) * P], in_=blocks(k_ps[:], H))

        def project_v(b):
            v_ps = psum.tile([P, C], F32, name="v_ps", tag="mm", bufs=4)
            for cb in range(CB):
                nc.tensor.matmul(
                    v_ps[:],
                    lhsT=x_blk[b][:, cb * P : (cb + 1) * P],
                    rhs=wv_sb[:, cb * C : (cb + 1) * C],
                    start=(cb == 0),
                    stop=(cb == CB - 1),
                )
            nc.vector.tensor_tensor(
                out=vT_sb[:, b * C : (b + 1) * C], in0=v_ps[:], in1=bv_row[:], op=ALU.add
            )

        def scores(b, n):
            seen = (b + 1) * P
            q_head = q_blk[b][:, n * P : (n + 1) * P]
            neg_s[b, n] = work.tile([P, N], F32, name="neg_s", bufs=3)
            neg_max[b, n] = None
            s_banks[b, n] = []
            for lo in range(0, seen, BANK):
                hi = min(lo + BANK, seen)
                s_ps = psum.tile([P, BANK], F32, name="s_ps", tag="mm", bufs=4)
                s_banks[b, n].append((lo, hi, s_ps))
                before_diag = min(hi, seen - P)
                if before_diag > lo:
                    nc.tensor.matmul(
                        s_ps[:, 0 : before_diag - lo],
                        lhsT=q_head,
                        rhs=k_sb[:, n * N + lo : n * N + before_diag],
                        start=True,
                        stop=True,
                    )
                if hi == seen:
                    diag = s_ps[:, seen - P - lo : seen - lo]
                    nc.tensor.matmul(
                        diag,
                        lhsT=q_head,
                        rhs=k_sb[:, n * N + seen - P : n * N + seen],
                        start=True,
                        stop=False,
                    )
                    nc.tensor.matmul(diag, lhsT=ident_b[:], rhs=causal[:], start=False, stop=True)

        def move_scores(b, n, bank):
            if bank < len(s_banks[b, n]):
                lo, hi, s_ps = s_banks[b, n][bank]
                smallest = small.tile([P, 1], F32, name="smallest", bufs=8)
                nc.vector.tensor_scalar(
                    out=neg_s[b, n][:, lo:hi],
                    in0=s_ps[:, 0 : hi - lo],
                    scalar1=-SCORE_SCALE,
                    scalar2=neg_max[b, n],
                    op0=ALU.mult,
                    op1=ALU.min,
                    accum_out=smallest[:],
                )
                neg_max[b, n] = smallest[:]

        def exponentials(b, n):
            seen = (b + 1) * P
            if n == 0:
                row_sum[b] = small.tile([P, H], F32, name="row_sum")
            p_sb[b, n] = work.tile([P, N], BF16, name="p_sb", bufs=4)
            nc.scalar.activation(
                out=p_sb[b, n][:, 0:seen],
                in_=neg_s[b, n][:, 0:seen],
                func=ACT.Exp,
                bias=neg_max[b, n],
                scale=-1.0,
                accum_out=row_sum[b][:, n : n + 1],
            )

        def keys_to_partitions(b, n):
            seen = (b + 1) * P
            pT_ps = psum.tile([P, N], BF16, name="pT_ps", tag="flip")
            for ib in range(b + 1):
                part = slice(ib * P, (ib + 1) * P)
                nc.tensor.transpose(out=pT_ps[:, part], in_=p_sb[b, n][:, part], identity=ident_b[:])
            pT_sb[b, n] = work.tile([P, N], BF16, name="pT_sb", bufs=3)
            if n % 2 == 0:
                nc.scalar.copy(out=pT_sb[b, n][:, 0:seen], in_=pT_ps[:, 0:seen])
            else:
                nc.vector.tensor_copy(out=pT_sb[b, n][:, 0:seen], in_=pT_ps[:, 0:seen])

        def weighted_sum(b, n):
            if n == 0:
                oT_ps[b] = psum.tile([P, C], F32, name="oT_ps", tag="acc")
            for ib in range(b + 1):
                nc.tensor.matmul(
                    oT_ps[b][:, n * P : (n + 1) * P],
                    lhsT=pT_sb[b, n][:, ib * P : (ib + 1) * P],
                    rhs=vT_sb[:, ib * C + n * P : ib * C + (n + 1) * P],
                    start=(ib == 0),
                    stop=(ib == b),
                )

        def divide_and_gate(b):
            inv_sum = small.tile([P, H], F32, name="inv_sum")
            nc.vector.reciprocal(out=inv_sum[:], in_=row_sum[b][:])
            head_scale = small.tile([P, H], F32, name="head_scale")
            nc.vector.tensor_tensor(out=head_scale[:], in0=inv_sum[:], in1=gate_col, op=ALU.mult)
            oT_sb[b] = work.tile([P, C], BF16, name="oT_sb")
            for n in range(H):
                part = slice(n * P, (n + 1) * P)
                nc.scalar.activation(
                    out=oT_sb[b][:, part],
                    in_=oT_ps[b][:, part],
                    func=ACT.Identity,
                    scale=head_scale[:, n : n + 1],
                )

        def channels_to_partitions(b):
            o_ps = psum.tile([P, C], BF16, name="o_ps", tag="flip")
            for n in range(H):
                part = slice(n * P, (n + 1) * P)
                nc.tensor.transpose(out=o_ps[:, part], in_=oT_sb[b][:, part], identity=ident_b[:])
            o_sb[b] = work.tile([P, C], BF16, name="o_sb")
            nc.vector.tensor_copy(out=o_sb[b][:], in_=o_ps[:])

        def project_out(b):
            y_ps[b] = psum.tile([P, C], F32, name="y_ps", tag="acc")
            for cb in range(CB):
                for n in range(H):
                    nc.tensor.matmul(
                        y_ps[b][:, cb * P : (cb + 1) * P],
                        lhsT=wo_sb[:, n * C + cb * P : n * C + (cb + 1) * P],
                        rhs=o_sb[b][:, n * P : (n + 1) * P],
                        start=(n == 0),
                        stop=(n == H - 1),
                    )

        def residual_and_store(b):
            tokens = slice(b * P, (b + 1) * P)
            y_sb = work.tile([P, C], F32, name="y_sb")
            nc.vector.tensor_tensor(
                out=blocks(y_sb[:], CB),
                in0=blocks(y_ps[b][:], CB),
                in1=blocks(h_sb[:], CB)[:, :, tokens],
                op=ALU.add,
            )
            nc.sync.dma_start(
                out.rearrange("(a p) j -> p a j", p=P)[:, :, tokens], blocks(y_sb[:], CB)
            )

        def block_head(step):
            return divmod(step, H) if 0 <= step < JB * H else None

        def layer_norm_part(b, part):
            if part == 0:
                look_up_block(b)
            if part == 1:
                token_statistics(b)
            if part == 2:
                normalise(b)
            if part == 3:
                gain_and_bias(b)

        for part in range(4):
            for b in range(LEAD):
                layer_norm_part(b, part)

        END_LAG = 7
        for step in range(-H, JB * H + END_LAG):
            b, n = divmod(step, H)
            if block_head(step):
                scores(b, n)
                move_scores(b, n, 0)
            if block_head(step - 2):
                keys_to_partitions(*block_head(step - 2))
            if block_head(step):
                move_scores(b, n, 1)
            if LEAD <= b + LEAD < JB:
                layer_norm_part(b + LEAD, n)
            if 0 <= b + 1 < JB:
                if n == 0:
                    project_q(b + 1)
                if n == 1:
                    project_k(b + 1)
                if n == 2:
                    project_v(b + 1)
            if block_head(step):
                exponentials(b, n)
            if block_head(step - END_LAG):
                ended, part = block_head(step - END_LAG)
                if part == 0:
                    divide_and_gate(ended)
                if part == 1:
                    channels_to_partitions(ended)
                if part == 2:
                    project_out(ended)
                if part == 3:
                    residual_and_store(ended)
            if block_head(step - 3):
                weighted_sum(*block_head(step - 3))
